import numpy as np
import ml_dtypes


def mxq(x, axis, fmt="e4m3"):
    dtype, down = {"e4m3": (ml_dtypes.float8_e4m3fn, 7), "e5m2": (ml_dtypes.float8_e5m2, 14)}[fmt]
    v = np.moveaxis(np.asarray(x, np.float32).astype(ml_dtypes.bfloat16).astype(np.float64), axis, -1)
    blocks = v.reshape(v.shape[:-1] + (-1, 32))
    amax = np.abs(blocks).max(-1, keepdims=True)
    byte = np.maximum(np.where(amax > 0, np.frexp(amax)[1] - 1 + 127, 0) - down, 1)
    scale = np.exp2(byte - 127.0)
    codes = (blocks / scale).astype(np.float32).astype(dtype).astype(np.float64)
    return np.moveaxis((codes * scale).reshape(v.shape), -1, axis)


WIDE = False


def mx_kscale(k):
    if not WIDE:
        return np.ones(k)
    levels = np.array([10, -10, 5, -5, 0])
    a = np.random.permutation(np.resize(levels, k // 512 * 4)).reshape(k // 512, 4)
    idx = np.arange(k)
    return np.exp2(a[idx // 512, idx % 128 // 32])


BF16 = ml_dtypes.bfloat16


def bf(x):
    return np.asarray(x, np.float32).astype(BF16)


def f64(x):
    return np.asarray(x).astype(np.float64)


B, N, D, F, H = 1, 1024, 1024, 1024, 16
DH = F // H
EPS = 1e-12


def l2norm(t):
    nrm = np.sqrt(np.sum(t * t, axis=-1, keepdims=True))
    return t / np.maximum(nrm, EPS)


def setup_inputs():
    s = mx_kscale(D)
    return {"x": bf(np.random.standard_normal((B, N, D)) * s),
            "Wq": bf(np.random.standard_normal((D, F)) / np.sqrt(D) / s[:, None]),
            "Wk": bf(np.random.standard_normal((D, F)) / np.sqrt(D) / s[:, None])}


def reference(x, Wq, Wk):
    xq = mxq(f64(x), 2, "e4m3")

    def heads(W):
        y = xq @ mxq(f64(W), 0, "e4m3")
        return y.reshape(B, N, H, DH).transpose(0, 2, 1, 3)

    return l2norm(heads(Wq)), l2norm(heads(Wk))

@@ -1,0 +1,210 @@
+from contextlib import ExitStack
+
+import concourse.mybir as mybir
+from concourse.masks import make_identity
+
+F32 = mybir.dt.float32
+BF16 = mybir.dt.bfloat16
+U32 = mybir.dt.uint32
+U8 = mybir.dt.uint8
+FP8X4 = mybir.dt.float8_e4m3fn_x4
+ACT = mybir.ActivationFunctionType
+ALU = mybir.AluOpType
+
+P = 128
+PACK = 4
+K_PASS = P * PACK
+
+TOKENS = 1024
+D_IN = 1024
+FEATURES = 1024
+HEAD_DIM = 64
+EPS = 1e-12
+
+PASSES = D_IN // K_PASS
+TOKEN_TILES = TOKENS // P
+BANK = 512
+HEADS_PER_CHUNK = BANK // HEAD_DIM
+CHUNKS_PER_WEIGHT = FEATURES // BANK
+CHUNKS = 2 * CHUNKS_PER_WEIGHT
+PAIR = 2
+PAIRS = TOKEN_TILES // PAIR
+UNITS = CHUNKS * PAIRS
+QUARTER = PASSES * BANK // PAIRS
+TOKEN_TILES_PER_STORE = 4
+WORDS = D_IN // 2
+
+FLOPS = 2 * TOKENS * D_IN * 2 * FEATURES
+
+
+def tile_attention_pa_kernel(tc, x, Wq, Wk, out_0, out_1):
+    nc = tc.nc
+    weights = (Wq, Wk)
+    x_rows = x.flatten_outer_dims().rearrange("(p m) d -> p (m d)", m=TOKEN_TILES)
+    out_views = [
+        out.rearrange("b h (p m) d -> p (b h) m d", m=TOKEN_TILES) for out in (out_0, out_1)
+    ]
+
+    with ExitStack() as ctx:
+        keep = ctx.enter_context(tc.tile_pool(name="keep", bufs=1))
+        grouped_pool = ctx.enter_context(tc.tile_pool(name="grouped", bufs=4))
+        scratch_pool = ctx.enter_context(tc.tile_pool(name="scratch", bufs=3))
+        small_pool = ctx.enter_context(tc.tile_pool(name="small", bufs=4))
+        result_pool = ctx.enter_context(tc.tile_pool(name="result", bufs=3))
+        psum = ctx.enter_context(tc.psum_pool(name="psum", bufs=4))
+
+        x_sb = keep.tile([P, TOKEN_TILES * D_IN], BF16, name="x_sb")
+        for pair in range(PAIRS):
+            cols = slice(pair * PAIR * D_IN, (pair + 1) * PAIR * D_IN)
+            nc.sync.dma_start(out=x_sb[:, cols], in_=x_rows[:, cols])
+        w_raw = keep.tile([P, CHUNKS, PASSES, PACK, BANK], BF16, name="w_raw")
+        for n in range(CHUNKS):
+            w = weights[n // CHUNKS_PER_WEIGHT]
+            c0 = (n % CHUNKS_PER_WEIGHT) * BANK
+            for g in range(PASSES):
+                nc.sync.dma_start(
+                    out=w_raw[:, n, g, :, :],
+                    in_=w[g * K_PASS : (g + 1) * K_PASS, c0 : c0 + BANK].rearrange(
+                        "(p t) c -> p t c", t=PACK
+                    ),
+                )
+
+        one = keep.tile([P, 1], F32, name="one")
+        nc.vector.memset(one[:], 1.0)
+        warm = keep.tile([P, 1], F32, name="warm")
+        nc.scalar.activation(out=warm[:], in_=one[:], func=ACT.Abs_reciprocal_sqrt)
+
+        ident = keep.tile([P, P], F32, name="ident")
+        make_identity(nc, ident[:])
+
+        x_words = x_sb[:].bitcast(F32)
+        x_grouped = keep.tile([P, TOKEN_TILES * D_IN], BF16, name="x_grouped", align_bytes=64)
+        x_grouped_words = x_grouped[:].bitcast(F32)
+        x_codes = keep.tile([P, TOKEN_TILES * PASSES * P], U32, name="x_codes", align_bytes=64)
+        x_scales = keep.tile([P, TOKEN_TILES * PASSES * P], U8, name="x_scales", align_bytes=64)
+        for pair in range(PAIRS):
+            xt = psum.tile([P, PAIR, BANK], F32, tag="banks")
+            for b in range(PAIR):
+                m = pair * PAIR + b
+                for g in range(PASSES):
+                    for u in range(2):
+                        nc.tensor.transpose(
+                            xt[:, b, (2 * g + u) * P : (2 * g + u + 1) * P],
+                            x_words[:, m * WORDS + 2 * P * g + u : m * WORDS + 2 * P * (g + 1) : 2],
+                            ident[:],
+                        )
+                nc.scalar.copy(
+                    out=x_grouped_words[:, m * WORDS : (m + 1) * WORDS].rearrange(
+                        "p (g r u) -> p g r u", g=PASSES, u=2
+                    ),
+                    in_=xt[:, b, :].rearrange("p (g u r) -> p g r u", g=PASSES, u=2),
+                )
+            nc.vector.quantize_mx(
+                out=x_codes[:, pair * PAIR * PASSES * P : (pair + 1) * PAIR * PASSES * P].bitcast(FP8X4),
+                scales=x_scales[:, pair * PAIR * PASSES * P : (pair + 1) * PAIR * PASSES * P],
+                in_=x_grouped[:, pair * PAIR * D_IN : (pair + 1) * PAIR * D_IN],
+            )
+
+        w_codes = keep.tile([P, CHUNKS, PASSES, BANK], U32, name="w_codes", align_bytes=64)
+        w_scales = keep.tile([P, CHUNKS, PASSES, BANK], U8, name="w_scales", align_bytes=64)
+
+        def regroup_weights(n, quarter):
+            g = quarter * QUARTER // BANK
+            c0 = quarter * QUARTER % BANK
+            grouped = grouped_pool.tile([P, QUARTER, PACK], BF16, align_bytes=64)
+            nc.vector.tensor_copy(
+                out=grouped[:].rearrange("p (c i) t -> p c t i", i=4),
+                in_=w_raw[:, n, g, :, c0 : c0 + QUARTER].rearrange("p t (c i) -> p c t i", i=4),
+            )
+            return grouped
+
+        def quantise_weights(n, quarter, grouped):
+            g = quarter * QUARTER // BANK
+            c0 = quarter * QUARTER % BANK
+            nc.vector.quantize_mx(
+                out=w_codes[:, n, g, c0 : c0 + QUARTER].bitcast(FP8X4),
+                scales=w_scales[:, n, g, c0 : c0 + QUARTER],
+                in_=grouped[:].rearrange("p c t -> p (c t)"),
+            )
+
+        first_grouped = [regroup_weights(0, quarter) for quarter in range(PAIRS)]
+        for quarter in range(PAIRS):
+            quantise_weights(0, quarter, first_grouped[quarter])
+
+        def project(n, pair):
+            acc = psum.tile([P, PAIR, BANK], F32, tag="banks")
+            for b in range(PAIR):
+                m = pair * PAIR + b
+                for g in range(PASSES):
+                    tokens = slice((m * PASSES + g) * P, (m * PASSES + g + 1) * P)
+                    nc.tensor.matmul_mx(
+                        out=acc[:, b, :],
+                        lhsT=x_codes[:, tokens].bitcast(FP8X4),
+                        lhsT_scale=x_scales[:, tokens],
+                        rhs=w_codes[:, n, g, :].bitcast(FP8X4),
+                        rhs_scale=w_scales[:, n, g, :],
+                        start=(g == 0),
+                        stop=(g == PASSES - 1),
+                    )
+            return acc
+
+        def sums_of_squares(acc):
+            squares = scratch_pool.tile([P, PAIR, BANK], BF16)
+            sumsq = small_pool.tile([P, PAIR * HEADS_PER_CHUNK], F32)
+            for b in range(PAIR):
+                for h in range(HEADS_PER_CHUNK):
+                    nc.scalar.activation(
+                        out=squares[:, b, h * HEAD_DIM : (h + 1) * HEAD_DIM],
+                        in_=acc[:, b, h * HEAD_DIM : (h + 1) * HEAD_DIM],
+                        func=ACT.Square,
+                        accum_out=sumsq[:, b * HEADS_PER_CHUNK + h : b * HEADS_PER_CHUNK + h + 1],
+                    )
+            return sumsq
+
+        def normalise(pair, acc, sumsq, result):
+            inv_norm = small_pool.tile([P, PAIR * HEADS_PER_CHUNK], F32)
+            nc.scalar.activation(out=inv_norm[:], in_=sumsq[:], func=ACT.Abs_reciprocal_sqrt)
+            for b in range(PAIR):
+                nc.vector.scalar_tensor_tensor(
+                    out=result[:, :, pair * PAIR + b, :],
+                    in0=inv_norm[:, b * HEADS_PER_CHUNK : (b + 1) * HEADS_PER_CHUNK]
+                    .unsqueeze(2)
+                    .to_broadcast([P, HEADS_PER_CHUNK, HEAD_DIM]),
+                    scalar=1.0 / EPS,
+                    in1=acc[:, b, :].rearrange("p (h d) -> p h d", d=HEAD_DIM),
+                    op0=ALU.min,
+                    op1=ALU.mult,
+                )
+
+        def store(n, pair, result):
+            m1 = (pair + 1) * PAIR
+            if m1 % TOKEN_TILES_PER_STORE == 0:
+                h0 = (n % CHUNKS_PER_WEIGHT) * HEADS_PER_CHUNK
+                nc.sync.dma_start(
+                    out=out_views[n // CHUNKS_PER_WEIGHT][
+                        :, h0 : h0 + HEADS_PER_CHUNK, m1 - TOKEN_TILES_PER_STORE : m1, :
+                    ],
+                    in_=result[:, :, m1 - TOKEN_TILES_PER_STORE : m1, :],
+                )
+
+        units = []
+        result = None
+        for unit in range(UNITS + 1):
+            n, pair = divmod(unit, PAIRS)
+            grouped = None
+            if unit < UNITS:
+                if pair == 0:
+                    result = result_pool.tile(
+                        [P, HEADS_PER_CHUNK, TOKEN_TILES, HEAD_DIM], F32, name="result"
+                    )
+                acc = project(n, pair)
+                sumsq = sums_of_squares(acc)
+                units.append((n, pair, acc, sumsq, result))
+                if n + 1 < CHUNKS:
+                    grouped = regroup_weights(n + 1, pair)
+            if unit > 0:
+                old_n, old_pair, old_acc, old_sumsq, old_result = units[unit - 1]
+                normalise(old_pair, old_acc, old_sumsq, old_result)
+                store(old_n, old_pair, old_result)
+            if grouped is not None:
+                quantise_weights(n + 1, pair, grouped)

@@ -54,11 +54,9 @@ def tile_attention_pa_kernel(tc, x, Wq, Wk, out_0, out_1):
         psum = ctx.enter_context(tc.psum_pool(name="psum", bufs=4))
 
         x_sb = keep.tile([P, TOKEN_TILES * D_IN], BF16, name="x_sb")
-        for pair in range(PAIRS):
-            cols = slice(pair * PAIR * D_IN, (pair + 1) * PAIR * D_IN)
-            nc.sync.dma_start(out=x_sb[:, cols], in_=x_rows[:, cols])
         w_raw = keep.tile([P, CHUNKS, PASSES, PACK, BANK], BF16, name="w_raw")
-        for n in range(CHUNKS):
+
+        def load_weights(n):
             w = weights[n // CHUNKS_PER_WEIGHT]
             c0 = (n % CHUNKS_PER_WEIGHT) * BANK
             for g in range(PASSES):
@@ -69,6 +67,13 @@ def tile_attention_pa_kernel(tc, x, Wq, Wk, out_0, out_1):
                     ),
                 )
 
+        load_weights(0)
+        for pair in range(PAIRS):
+            cols = slice(pair * PAIR * D_IN, (pair + 1) * PAIR * D_IN)
+            nc.sync.dma_start(out=x_sb[:, cols], in_=x_rows[:, cols])
+        for n in range(1, CHUNKS):
+            load_weights(n)
+
         one = keep.tile([P, 1], F32, name="one")
         nc.vector.memset(one[:], 1.0)
         warm = keep.tile([P, 1], F32, name="warm")
@@ -76,6 +81,34 @@ def tile_attention_pa_kernel(tc, x, Wq, Wk, out_0, out_1):
 
         ident = keep.tile([P, P], F32, name="ident")
         make_identity(nc, ident[:])
+
+        w_codes = keep.tile([P, CHUNKS, PASSES, BANK], U32, name="w_codes", align_bytes=64)
+        w_scales = keep.tile([P, CHUNKS, PASSES, BANK], U8, name="w_scales", align_bytes=64)
+
+        def regroup_weights(n, quarter, on_scalar=False):
+            g = quarter * QUARTER // BANK
+            c0 = quarter * QUARTER % BANK
+            grouped = grouped_pool.tile([P, QUARTER, PACK], BF16, align_bytes=64, name="grouped")
+            dst = grouped[:].rearrange("p (c i) t -> p c t i", i=4)
+            rows = w_raw[:, n, g, :, c0 : c0 + QUARTER].rearrange("p t (c i) -> p c t i", i=4)
+            if on_scalar:
+                nc.scalar.copy(out=dst, in_=rows)
+            else:
+                nc.vector.tensor_copy(out=dst, in_=rows)
+            return grouped
+
+        def quantise_weights(n, quarter, grouped):
+            g = quarter * QUARTER // BANK
+            c0 = quarter * QUARTER % BANK
+            nc.vector.quantize_mx(
+                out=w_codes[:, n, g, c0 : c0 + QUARTER].bitcast(FP8X4),
+                scales=w_scales[:, n, g, c0 : c0 + QUARTER],
+                in_=grouped[:].rearrange("p c t -> p (c t)"),
+            )
+
+        first_grouped = [
+            regroup_weights(0, quarter, on_scalar=(quarter == PAIRS - 1)) for quarter in range(PAIRS)
+        ]
 
         x_words = x_sb[:].bitcast(F32)
         x_grouped = keep.tile([P, TOKEN_TILES * D_IN], BF16, name="x_grouped", align_bytes=64)
@@ -99,37 +132,18 @@ def tile_attention_pa_kernel(tc, x, Wq, Wk, out_0, out_1):
                     ),
                     in_=xt[:, b, :].rearrange("p (g u r) -> p g r u", g=PASSES, u=2),
                 )
+
+        def quantise_x(pair):
             nc.vector.quantize_mx(
                 out=x_codes[:, pair * PAIR * PASSES * P : (pair + 1) * PAIR * PASSES * P].bitcast(FP8X4),
                 scales=x_scales[:, pair * PAIR * PASSES * P : (pair + 1) * PAIR * PASSES * P],
                 in_=x_grouped[:, pair * PAIR * D_IN : (pair + 1) * PAIR * D_IN],
             )
 
-        w_codes = keep.tile([P, CHUNKS, PASSES, BANK], U32, name="w_codes", align_bytes=64)
-        w_scales = keep.tile([P, CHUNKS, PASSES, BANK], U8, name="w_scales", align_bytes=64)
-
-        def regroup_weights(n, quarter):
-            g = quarter * QUARTER // BANK
-            c0 = quarter * QUARTER % BANK
-            grouped = grouped_pool.tile([P, QUARTER, PACK], BF16, align_bytes=64)
-            nc.vector.tensor_copy(
-                out=grouped[:].rearrange("p (c i) t -> p c t i", i=4),
-                in_=w_raw[:, n, g, :, c0 : c0 + QUARTER].rearrange("p t (c i) -> p c t i", i=4),
-            )
-            return grouped
-
-        def quantise_weights(n, quarter, grouped):
-            g = quarter * QUARTER // BANK
-            c0 = quarter * QUARTER % BANK
-            nc.vector.quantize_mx(
-                out=w_codes[:, n, g, c0 : c0 + QUARTER].bitcast(FP8X4),
-                scales=w_scales[:, n, g, c0 : c0 + QUARTER],
-                in_=grouped[:].rearrange("p c t -> p (c t)"),
-            )
-
-        first_grouped = [regroup_weights(0, quarter) for quarter in range(PAIRS)]
         for quarter in range(PAIRS):
             quantise_weights(0, quarter, first_grouped[quarter])
+        for pair in range(PAIRS):
+            quantise_x(pair)
 
         def project(n, pair):
             acc = psum.tile([P, PAIR, BANK], F32, tag="banks")

@@ -51,7 +51,7 @@ def tile_attention_pa_kernel(tc, x, Wq, Wk, out_0, out_1):
         scratch_pool = ctx.enter_context(tc.tile_pool(name="scratch", bufs=3))
         small_pool = ctx.enter_context(tc.tile_pool(name="small", bufs=4))
         result_pool = ctx.enter_context(tc.tile_pool(name="result", bufs=3))
-        psum = ctx.enter_context(tc.psum_pool(name="psum", bufs=4))
+        psum = ctx.enter_context(tc.psum_pool(name="psum", bufs=8))
 
         x_sb = keep.tile([P, TOKEN_TILES * D_IN], BF16, name="x_sb")
         w_raw = keep.tile([P, CHUNKS, PASSES, PACK, BANK], BF16, name="w_raw")
@@ -116,13 +116,13 @@ def tile_attention_pa_kernel(tc, x, Wq, Wk, out_0, out_1):
         x_codes = keep.tile([P, TOKEN_TILES * PASSES * P], U32, name="x_codes", align_bytes=64)
         x_scales = keep.tile([P, TOKEN_TILES * PASSES * P], U8, name="x_scales", align_bytes=64)
         for pair in range(PAIRS):
-            xt = psum.tile([P, PAIR, BANK], F32, tag="banks")
             for b in range(PAIR):
+                xt = psum.tile([P, BANK], F32, tag="bank", name="xt")
                 m = pair * PAIR + b
                 for g in range(PASSES):
                     for u in range(2):
                         nc.tensor.transpose(
-                            xt[:, b, (2 * g + u) * P : (2 * g + u + 1) * P],
+                            xt[:, (2 * g + u) * P : (2 * g + u + 1) * P],
                             x_words[:, m * WORDS + 2 * P * g + u : m * WORDS + 2 * P * (g + 1) : 2],
                             ident[:],
                         )
@@ -130,7 +130,7 @@ def tile_attention_pa_kernel(tc, x, Wq, Wk, out_0, out_1):
                     out=x_grouped_words[:, m * WORDS : (m + 1) * WORDS].rearrange(
                         "p (g r u) -> p g r u", g=PASSES, u=2
                     ),
-                    in_=xt[:, b, :].rearrange("p (g u r) -> p g r u", g=PASSES, u=2),
+                    in_=xt[:].rearrange("p (g u r) -> p g r u", g=PASSES, u=2),
                 )
 
         def quantise_x(pair):
@@ -145,50 +145,46 @@ def tile_attention_pa_kernel(tc, x, Wq, Wk, out_0, out_1):
         for pair in range(PAIRS):
             quantise_x(pair)
 
-        def project(n, pair):
-            acc = psum.tile([P, PAIR, BANK], F32, tag="banks")
-            for b in range(PAIR):
-                m = pair * PAIR + b
-                for g in range(PASSES):
-                    tokens = slice((m * PASSES + g) * P, (m * PASSES + g + 1) * P)
-                    nc.tensor.matmul_mx(
-                        out=acc[:, b, :],
-                        lhsT=x_codes[:, tokens].bitcast(FP8X4),
-                        lhsT_scale=x_scales[:, tokens],
-                        rhs=w_codes[:, n, g, :].bitcast(FP8X4),
-                        rhs_scale=w_scales[:, n, g, :],
-                        start=(g == 0),
-                        stop=(g == PASSES - 1),
-                    )
+        def project(n, m):
+            acc = psum.tile([P, BANK], F32, tag="bank", name="acc")
+            for g in range(PASSES):
+                tokens = slice((m * PASSES + g) * P, (m * PASSES + g + 1) * P)
+                nc.tensor.matmul_mx(
+                    out=acc[:],
+                    lhsT=x_codes[:, tokens].bitcast(FP8X4),
+                    lhsT_scale=x_scales[:, tokens],
+                    rhs=w_codes[:, n, g, :].bitcast(FP8X4),
+                    rhs_scale=w_scales[:, n, g, :],
+                    start=(g == 0),
+                    stop=(g == PASSES - 1),
+                )
             return acc
 
-        def sums_of_squares(acc):
-            squares = scratch_pool.tile([P, PAIR, BANK], BF16)
-            sumsq = small_pool.tile([P, PAIR * HEADS_PER_CHUNK], F32)
-            for b in range(PAIR):
-                for h in range(HEADS_PER_CHUNK):
-                    nc.scalar.activation(
-                        out=squares[:, b, h * HEAD_DIM : (h + 1) * HEAD_DIM],
-                        in_=acc[:, b, h * HEAD_DIM : (h + 1) * HEAD_DIM],
-                        func=ACT.Square,
-                        accum_out=sumsq[:, b * HEADS_PER_CHUNK + h : b * HEADS_PER_CHUNK + h + 1],
-                    )
-            return sumsq
-
-        def normalise(pair, acc, sumsq, result):
-            inv_norm = small_pool.tile([P, PAIR * HEADS_PER_CHUNK], F32)
-            nc.scalar.activation(out=inv_norm[:], in_=sumsq[:], func=ACT.Abs_reciprocal_sqrt)
-            for b in range(PAIR):
-                nc.vector.scalar_tensor_tensor(
-                    out=result[:, :, pair * PAIR + b, :],
-                    in0=inv_norm[:, b * HEADS_PER_CHUNK : (b + 1) * HEADS_PER_CHUNK]
-                    .unsqueeze(2)
-                    .to_broadcast([P, HEADS_PER_CHUNK, HEAD_DIM]),
-                    scalar=1.0 / EPS,
-                    in1=acc[:, b, :].rearrange("p (h d) -> p h d", d=HEAD_DIM),
-                    op0=ALU.min,
-                    op1=ALU.mult,
+        def sums_of_squares(acc, b, sumsq, squares):
+            for h in range(HEADS_PER_CHUNK):
+                nc.scalar.activation(
+                    out=squares[:, b, h * HEAD_DIM : (h + 1) * HEAD_DIM],
+                    in_=acc[:, h * HEAD_DIM : (h + 1) * HEAD_DIM],
+                    func=ACT.Square,
+                    accum_out=sumsq[:, b * HEADS_PER_CHUNK + h : b * HEADS_PER_CHUNK + h + 1],
                 )
+
+        def inverse_norms(sumsq):
+            inv_norm = small_pool.tile([P, PAIR * HEADS_PER_CHUNK], F32, name="inv_norm")
+            nc.scalar.activation(out=inv_norm[:], in_=sumsq[:], func=ACT.Abs_reciprocal_sqrt)
+            return inv_norm
+
+        def scale(pair, b, acc, inv_norm, result):
+            nc.vector.scalar_tensor_tensor(
+                out=result[:, :, pair * PAIR + b, :],
+                in0=inv_norm[:, b * HEADS_PER_CHUNK : (b + 1) * HEADS_PER_CHUNK]
+                .unsqueeze(2)
+                .to_broadcast([P, HEADS_PER_CHUNK, HEAD_DIM]),
+                scalar=1.0 / EPS,
+                in1=acc[:].rearrange("p (h d) -> p h d", d=HEAD_DIM),
+                op0=ALU.min,
+                op1=ALU.mult,
+            )
 
         def store(n, pair, result):
             m1 = (pair + 1) * PAIR
@@ -211,14 +207,21 @@ def tile_attention_pa_kernel(tc, x, Wq, Wk, out_0, out_1):
                     result = result_pool.tile(
                         [P, HEADS_PER_CHUNK, TOKEN_TILES, HEAD_DIM], F32, name="result"
                     )
-                acc = project(n, pair)
-                sumsq = sums_of_squares(acc)
-                units.append((n, pair, acc, sumsq, result))
+                accs = [project(n, pair * PAIR + b) for b in range(PAIR)]
+                squares = scratch_pool.tile([P, PAIR, BANK], BF16, name="squares")
+                sumsq = small_pool.tile([P, PAIR * HEADS_PER_CHUNK], F32, name="sumsq")
+                units.append((n, pair, accs, sumsq, result))
+                sums_of_squares(accs[0], 0, sumsq, squares)
+            if unit > 0:
+                old_n, old_pair, old_accs, old_sumsq, old_result = units[unit - 1]
+                old_inv = inverse_norms(old_sumsq)
+                scale(old_pair, 0, old_accs[0], old_inv, old_result)
+            if unit < UNITS:
+                sums_of_squares(accs[1], 1, sumsq, squares)
                 if n + 1 < CHUNKS:
                     grouped = regroup_weights(n + 1, pair)
             if unit > 0:
-                old_n, old_pair, old_acc, old_sumsq, old_result = units[unit - 1]
-                normalise(old_pair, old_acc, old_sumsq, old_result)
+                scale(old_pair, 1, old_accs[1], old_inv, old_result)
                 store(old_n, old_pair, old_result)
             if grouped is not None:
                 quantise_weights(n + 1, pair, grouped)

@@ -10,6 +10,7 @@ U8 = mybir.dt.uint8
 FP8X4 = mybir.dt.float8_e4m3fn_x4
 ACT = mybir.ActivationFunctionType
 ALU = mybir.AluOpType
+AX = mybir.AxisListType
 
 P = 128
 PACK = 4
@@ -34,6 +35,8 @@ QUARTER = PASSES * BANK // PAIRS
 TOKEN_TILES_PER_STORE = 4
 WORDS = D_IN // 2
 
+SHARED_HEADS = 6
+
 FLOPS = 2 * TOKENS * D_IN * 2 * FEATURES
 
 
@@ -50,6 +53,7 @@ def tile_attention_pa_kernel(tc, x, Wq, Wk, out_0, out_1):
         grouped_pool = ctx.enter_context(tc.tile_pool(name="grouped", bufs=4))
         scratch_pool = ctx.enter_context(tc.tile_pool(name="scratch", bufs=3))
         small_pool = ctx.enter_context(tc.tile_pool(name="small", bufs=4))
+        wide_pool = ctx.enter_context(tc.tile_pool(name="wide", bufs=3))
         result_pool = ctx.enter_context(tc.tile_pool(name="result", bufs=3))
         psum = ctx.enter_context(tc.psum_pool(name="psum", bufs=8))
 
@@ -160,14 +164,24 @@ def tile_attention_pa_kernel(tc, x, Wq, Wk, out_0, out_1):
                 )
             return acc
 
-        def sums_of_squares(acc, b, sumsq, squares):
-            for h in range(HEADS_PER_CHUNK):
+        def sums_of_squares(acc, b, sumsq, squares, first=0):
+            for h in range(first, HEADS_PER_CHUNK):
                 nc.scalar.activation(
                     out=squares[:, b, h * HEAD_DIM : (h + 1) * HEAD_DIM],
                     in_=acc[:, h * HEAD_DIM : (h + 1) * HEAD_DIM],
                     func=ACT.Square,
                     accum_out=sumsq[:, b * HEADS_PER_CHUNK + h : b * HEADS_PER_CHUNK + h + 1],
                 )
+
+        def sums_of_squares_shared(acc, b, sumsq, heads):
+            squares_f32 = wide_pool.tile([P, heads * HEAD_DIM], F32, name="squares_f32")
+            nc.scalar.activation(out=squares_f32[:], in_=acc[:, : heads * HEAD_DIM], func=ACT.Square)
+            nc.vector.tensor_reduce(
+                out=sumsq[:, b * HEADS_PER_CHUNK : b * HEADS_PER_CHUNK + heads],
+                in_=squares_f32[:].rearrange("p (h d) -> p h d", d=HEAD_DIM),
+                axis=AX.X,
+                op=ALU.add,
+            )
 
         def inverse_norms(sumsq):
             inv_norm = small_pool.tile([P, PAIR * HEADS_PER_CHUNK], F32, name="inv_norm")
@@ -211,7 +225,11 @@ def tile_attention_pa_kernel(tc, x, Wq, Wk, out_0, out_1):
                 squares = scratch_pool.tile([P, PAIR, BANK], BF16, name="squares")
                 sumsq = small_pool.tile([P, PAIR * HEADS_PER_CHUNK], F32, name="sumsq")
                 units.append((n, pair, accs, sumsq, result))
-                sums_of_squares(accs[0], 0, sumsq, squares)
+                if n == CHUNKS - 1:
+                    sums_of_squares_shared(accs[0], 0, sumsq, SHARED_HEADS)
+                    sums_of_squares(accs[0], 0, sumsq, squares, SHARED_HEADS)
+                else:
+                    sums_of_squares(accs[0], 0, sumsq, squares)
             if unit > 0:
                 old_n, old_pair, old_accs, old_sumsq, old_result = units[unit - 1]
                 old_inv = inverse_norms(old_sumsq)

@@ -33,6 +33,7 @@ PAIRS = TOKEN_TILES // PAIR
 UNITS = CHUNKS * PAIRS
 QUARTER = PASSES * BANK // PAIRS
 TOKEN_TILES_PER_STORE = 4
+LEAD = 2
 WORDS = D_IN // 2
 
 SHARED_HEADS = 6
@@ -49,6 +50,7 @@ def tile_attention_pa_kernel(tc, x, Wq, Wk, out_0, out_1):
     ]
 
     with ExitStack() as ctx:
+        ctx.enter_context(tc.manual_schedule(engines={mybir.EngineType.DVE}))
         keep = ctx.enter_context(tc.tile_pool(name="keep", bufs=1))
         grouped_pool = ctx.enter_context(tc.tile_pool(name="grouped", bufs=4))
         scratch_pool = ctx.enter_context(tc.tile_pool(name="scratch", bufs=3))
@@ -211,11 +213,12 @@ def tile_attention_pa_kernel(tc, x, Wq, Wk, out_0, out_1):
                     in_=result[:, :, m1 - TOKEN_TILES_PER_STORE : m1, :],
                 )
 
+        quarters = [(n, quarter) for n in range(1, CHUNKS) for quarter in range(PAIRS)]
         units = []
         result = None
         for unit in range(UNITS + 1):
             n, pair = divmod(unit, PAIRS)
-            grouped = None
+            ready = quarters[:LEAD] if unit == 0 else quarters[unit + LEAD - 1 : unit + LEAD]
             if unit < UNITS:
                 if pair == 0:
                     result = result_pool.tile(
@@ -236,10 +239,10 @@ def tile_attention_pa_kernel(tc, x, Wq, Wk, out_0, out_1):
                 scale(old_pair, 0, old_accs[0], old_inv, old_result)
             if unit < UNITS:
                 sums_of_squares(accs[1], 1, sumsq, squares)
-                if n + 1 < CHUNKS:
-                    grouped = regroup_weights(n + 1, pair)
+                grouped = [regroup_weights(*q) for q in ready]
             if unit > 0:
                 scale(old_pair, 1, old_accs[1], old_inv, old_result)
                 store(old_n, old_pair, old_result)
-            if grouped is not None:
-                quantise_weights(n + 1, pair, grouped)
+            if unit < UNITS:
+                for q, tile in zip(ready, grouped):
+                    quantise_weights(*q, tile)

@@ -218,7 +218,7 @@ def tile_attention_pa_kernel(tc, x, Wq, Wk, out_0, out_1):
         result = None
         for unit in range(UNITS + 1):
             n, pair = divmod(unit, PAIRS)
-            ready = quarters[:LEAD] if unit == 0 else quarters[unit + LEAD - 1 : unit + LEAD]
+            ready = quarters[unit * LEAD : (unit + 1) * LEAD] if unit < LEAD else quarters[unit + LEAD : unit + LEAD + 1]
             if unit < UNITS:
                 if pair == 0:
                     result = result_pool.tile(

@@ -36,7 +36,15 @@ TOKEN_TILES_PER_STORE = 4
 LEAD = 2
 WORDS = D_IN // 2
 
-SHARED_HEADS = 6
+AHEAD = 2
+AHEAD_PARTS = 2
+VECTOR_QUARTERS = 3
+
+
+def shared_heads(unit):
+    if unit < 3:
+        return 0
+    return 5 if unit < UNITS - PAIRS else 6
 
 FLOPS = 2 * TOKENS * D_IN * 2 * FEATURES
 
@@ -53,6 +61,7 @@ def tile_attention_pa_kernel(tc, x, Wq, Wk, out_0, out_1):
         ctx.enter_context(tc.manual_schedule(engines={mybir.EngineType.DVE}))
         keep = ctx.enter_context(tc.tile_pool(name="keep", bufs=1))
         grouped_pool = ctx.enter_context(tc.tile_pool(name="grouped", bufs=4))
+        ahead_pool = ctx.enter_context(tc.tile_pool(name="ahead", bufs=AHEAD))
         scratch_pool = ctx.enter_context(tc.tile_pool(name="scratch", bufs=3))
         small_pool = ctx.enter_context(tc.tile_pool(name="small", bufs=4))
         wide_pool = ctx.enter_context(tc.tile_pool(name="wide", bufs=3))
@@ -90,6 +99,22 @@ def tile_attention_pa_kernel(tc, x, Wq, Wk, out_0, out_1):
 
         w_codes = keep.tile([P, CHUNKS, PASSES, BANK], U32, name="w_codes", align_bytes=64)
         w_scales = keep.tile([P, CHUNKS, PASSES, BANK], U8, name="w_scales", align_bytes=64)
+
+        def regroup_weights_ahead(n, quarter):
+            g = quarter * QUARTER // BANK
+            c0 = quarter * QUARTER % BANK
+            grouped = ahead_pool.tile([P, QUARTER, PACK], BF16, align_bytes=64, name="ahead")
+            width = QUARTER // AHEAD_PARTS
+            for c in range(0, QUARTER, width):
+                nc.gpsimd.tensor_scalar(
+                    out=grouped[:, c : c + width, :],
+                    in0=w_raw[:, n, g, :, c0 + c : c0 + c + width].rearrange("p t c -> p c t"),
+                    scalar1=1.0,
+                    scalar2=0.0,
+                    op0=ALU.mult,
+                    op1=ALU.add,
+                )
+            return grouped
 
         def regroup_weights(n, quarter, on_scalar=False):
             g = quarter * QUARTER // BANK
@@ -176,11 +201,12 @@ def tile_attention_pa_kernel(tc, x, Wq, Wk, out_0, out_1):
                 )
 
         def sums_of_squares_shared(acc, b, sumsq, heads):
-            squares_f32 = wide_pool.tile([P, heads * HEAD_DIM], F32, name="squares_f32")
-            nc.scalar.activation(out=squares_f32[:], in_=acc[:, : heads * HEAD_DIM], func=ACT.Square)
+            squares_f32 = wide_pool.tile([P, BANK], F32, name="squares_f32")
+            width = heads * HEAD_DIM
+            nc.scalar.activation(out=squares_f32[:, :width], in_=acc[:, :width], func=ACT.Square)
             nc.vector.tensor_reduce(
                 out=sumsq[:, b * HEADS_PER_CHUNK : b * HEADS_PER_CHUNK + heads],
-                in_=squares_f32[:].rearrange("p (h d) -> p h d", d=HEAD_DIM),
+                in_=squares_f32[:, :width].rearrange("p (h d) -> p h d", d=HEAD_DIM),
                 axis=AX.X,
                 op=ALU.add,
             )
@@ -214,11 +240,16 @@ def tile_attention_pa_kernel(tc, x, Wq, Wk, out_0, out_1):
                 )
 
         quarters = [(n, quarter) for n in range(1, CHUNKS) for quarter in range(PAIRS)]
+        grouped = {}
+        for i in range(VECTOR_QUARTERS, VECTOR_QUARTERS + AHEAD):
+            grouped[i] = regroup_weights_ahead(*quarters[i])
+
         units = []
         result = None
         for unit in range(UNITS + 1):
             n, pair = divmod(unit, PAIRS)
-            ready = quarters[unit * LEAD : (unit + 1) * LEAD] if unit < LEAD else quarters[unit + LEAD : unit + LEAD + 1]
+            ready = range(unit * LEAD, (unit + 1) * LEAD) if unit < LEAD else range(unit + LEAD, unit + LEAD + 1)
+            ready = [i for i in ready if i < len(quarters)]
             if unit < UNITS:
                 if pair == 0:
                     result = result_pool.tile(
@@ -228,21 +259,24 @@ def tile_attention_pa_kernel(tc, x, Wq, Wk, out_0, out_1):
                 squares = scratch_pool.tile([P, PAIR, BANK], BF16, name="squares")
                 sumsq = small_pool.tile([P, PAIR * HEADS_PER_CHUNK], F32, name="sumsq")
                 units.append((n, pair, accs, sumsq, result))
-                if n == CHUNKS - 1:
-                    sums_of_squares_shared(accs[0], 0, sumsq, SHARED_HEADS)
-                    sums_of_squares(accs[0], 0, sumsq, squares, SHARED_HEADS)
-                else:
-                    sums_of_squares(accs[0], 0, sumsq, squares)
+                shared = shared_heads(unit)
+                if shared:
+                    sums_of_squares_shared(accs[0], 0, sumsq, shared)
+                sums_of_squares(accs[0], 0, sumsq, squares, shared)
             if unit > 0:
                 old_n, old_pair, old_accs, old_sumsq, old_result = units[unit - 1]
                 old_inv = inverse_norms(old_sumsq)
                 scale(old_pair, 0, old_accs[0], old_inv, old_result)
             if unit < UNITS:
                 sums_of_squares(accs[1], 1, sumsq, squares)
-                grouped = [regroup_weights(*q) for q in ready]
+                for i in ready:
+                    if i < VECTOR_QUARTERS:
+                        grouped[i] = regroup_weights(*quarters[i])
             if unit > 0:
                 scale(old_pair, 1, old_accs[1], old_inv, old_result)
                 store(old_n, old_pair, old_result)
             if unit < UNITS:
-                for q, tile in zip(ready, grouped):
-                    quantise_weights(*q, tile)
+                for i in ready:
+                    quantise_weights(*quarters[i], grouped[i])
+                    if VECTOR_QUARTERS <= i < len(quarters) - AHEAD:
+                        grouped[i + AHEAD] = regroup_weights_ahead(*quarters[i + AHEAD])

@@ -25,26 +25,34 @@ EPS = 1e-12
 PASSES = D_IN // K_PASS
 TOKEN_TILES = TOKENS // P
 BANK = 512
-HEADS_PER_CHUNK = BANK // HEAD_DIM
-CHUNKS_PER_WEIGHT = FEATURES // BANK
+CHUNK = 512
+CHUNKS_PER_WEIGHT = FEATURES // CHUNK
 CHUNKS = 2 * CHUNKS_PER_WEIGHT
-PAIR = 2
+GROUP = 256
+GROUP_HEADS = GROUP // HEAD_DIM
+GROUPS_PER_WEIGHT = FEATURES // GROUP
+GROUPS = 2 * GROUPS_PER_WEIGHT
+GROUPS_PER_CHUNK = CHUNK // GROUP
+PAIR = BANK // GROUP
 PAIRS = TOKEN_TILES // PAIR
-UNITS = CHUNKS * PAIRS
-QUARTER = PASSES * BANK // PAIRS
-TOKEN_TILES_PER_STORE = 4
+SLOTS = PAIR * GROUP_HEADS
+SPAN = 4
+BANKS = SPAN // PAIR
+SPANS = TOKEN_TILES // SPAN
+UNITS = GROUPS * SPANS
 LEAD = 2
 WORDS = D_IN // 2
 
 AHEAD = 2
 AHEAD_PARTS = 2
-VECTOR_QUARTERS = 3
+VECTOR_PASSES = 3
 
 
 def shared_heads(unit):
     if unit < 3:
         return 0
-    return 5 if unit < UNITS - PAIRS else 6
+    return 4 if unit < UNITS - 4 else 6
+
 
 FLOPS = 2 * TOKENS * D_IN * 2 * FEATURES
 
@@ -65,19 +73,19 @@ def tile_attention_pa_kernel(tc, x, Wq, Wk, out_0, out_1):
         scratch_pool = ctx.enter_context(tc.tile_pool(name="scratch", bufs=3))
         small_pool = ctx.enter_context(tc.tile_pool(name="small", bufs=4))
         wide_pool = ctx.enter_context(tc.tile_pool(name="wide", bufs=3))
-        result_pool = ctx.enter_context(tc.tile_pool(name="result", bufs=3))
+        result_pool = ctx.enter_context(tc.tile_pool(name="result", bufs=6))
         psum = ctx.enter_context(tc.psum_pool(name="psum", bufs=8))
 
         x_sb = keep.tile([P, TOKEN_TILES * D_IN], BF16, name="x_sb")
-        w_raw = keep.tile([P, CHUNKS, PASSES, PACK, BANK], BF16, name="w_raw")
+        w_raw = keep.tile([P, CHUNKS, PASSES, PACK, CHUNK], BF16, name="w_raw")
 
-        def load_weights(n):
-            w = weights[n // CHUNKS_PER_WEIGHT]
-            c0 = (n % CHUNKS_PER_WEIGHT) * BANK
+        def load_weights(chunk):
+            w = weights[chunk // CHUNKS_PER_WEIGHT]
+            c0 = (chunk % CHUNKS_PER_WEIGHT) * CHUNK
             for g in range(PASSES):
                 nc.sync.dma_start(
-                    out=w_raw[:, n, g, :, :],
-                    in_=w[g * K_PASS : (g + 1) * K_PASS, c0 : c0 + BANK].rearrange(
+                    out=w_raw[:, chunk, g, :, :],
+                    in_=w[g * K_PASS : (g + 1) * K_PASS, c0 : c0 + CHUNK].rearrange(
                         "(p t) c -> p t c", t=PACK
                     ),
                 )
@@ -97,18 +105,21 @@ def tile_attention_pa_kernel(tc, x, Wq, Wk, out_0, out_1):
         ident = keep.tile([P, P], F32, name="ident")
         make_identity(nc, ident[:])
 
-        w_codes = keep.tile([P, CHUNKS, PASSES, BANK], U32, name="w_codes", align_bytes=64)
-        w_scales = keep.tile([P, CHUNKS, PASSES, BANK], U8, name="w_scales", align_bytes=64)
+        w_codes = keep.tile([P, GROUPS, PASSES, GROUP], U32, name="w_codes", align_bytes=64)
+        w_scales = keep.tile([P, GROUPS, PASSES, GROUP], U8, name="w_scales", align_bytes=64)
 
-        def regroup_weights_ahead(n, quarter):
-            g = quarter * QUARTER // BANK
-            c0 = quarter * QUARTER % BANK
-            grouped = ahead_pool.tile([P, QUARTER, PACK], BF16, align_bytes=64, name="ahead")
-            width = QUARTER // AHEAD_PARTS
-            for c in range(0, QUARTER, width):
+        def weight_rows(n, g):
+            c0 = (n % GROUPS_PER_CHUNK) * GROUP
+            return w_raw[:, n // GROUPS_PER_CHUNK, g, :, c0 : c0 + GROUP]
+
+        def regroup_weights_ahead(n, g):
+            rows = weight_rows(n, g)
+            grouped = ahead_pool.tile([P, GROUP, PACK], BF16, align_bytes=64, name="ahead")
+            width = GROUP // AHEAD_PARTS
+            for c in range(0, GROUP, width):
                 nc.gpsimd.tensor_scalar(
                     out=grouped[:, c : c + width, :],
-                    in0=w_raw[:, n, g, :, c0 + c : c0 + c + width].rearrange("p t c -> p c t"),
+                    in0=rows[:, :, c : c + width].rearrange("p t c -> p c t"),
                     scalar1=1.0,
                     scalar2=0.0,
                     op0=ALU.mult,
@@ -116,30 +127,25 @@ def tile_attention_pa_kernel(tc, x, Wq, Wk, out_0, out_1):
                 )
             return grouped
 
-        def regroup_weights(n, quarter, on_scalar=False):
-            g = quarter * QUARTER // BANK
-            c0 = quarter * QUARTER % BANK
-            grouped = grouped_pool.tile([P, QUARTER, PACK], BF16, align_bytes=64, name="grouped")
+        def regroup_weights(n, g, on_scalar=False):
+            grouped = grouped_pool.tile([P, GROUP, PACK], BF16, align_bytes=64, name="grouped")
             dst = grouped[:].rearrange("p (c i) t -> p c t i", i=4)
-            rows = w_raw[:, n, g, :, c0 : c0 + QUARTER].rearrange("p t (c i) -> p c t i", i=4)
+            rows = weight_rows(n, g).rearrange("p t (c i) -> p c t i", i=4)
             if on_scalar:
                 nc.scalar.copy(out=dst, in_=rows)
             else:
                 nc.vector.tensor_copy(out=dst, in_=rows)
             return grouped
 
-        def quantise_weights(n, quarter, grouped):
-            g = quarter * QUARTER // BANK
-            c0 = quarter * QUARTER % BANK
+        def quantise_weights(n, g, grouped):
             nc.vector.quantize_mx(
-                out=w_codes[:, n, g, c0 : c0 + QUARTER].bitcast(FP8X4),
-                scales=w_scales[:, n, g, c0 : c0 + QUARTER],
+                out=w_codes[:, n, g, :].bitcast(FP8X4),
+                scales=w_scales[:, n, g, :],
                 in_=grouped[:].rearrange("p c t -> p (c t)"),
             )
 
-        first_grouped = [
-            regroup_weights(0, quarter, on_scalar=(quarter == PAIRS - 1)) for quarter in range(PAIRS)
-        ]
+        first = [(n, g) for g in range(PASSES) for n in range(GROUPS_PER_CHUNK)]
+        first_grouped = [regroup_weights(n, g, on_scalar=((n, g) == first[-1])) for n, g in first]
 
         x_words = x_sb[:].bitcast(F32)
         x_grouped = keep.tile([P, TOKEN_TILES * D_IN], BF16, name="x_grouped", align_bytes=64)
@@ -171,112 +177,110 @@ def tile_attention_pa_kernel(tc, x, Wq, Wk, out_0, out_1):
                 in_=x_grouped[:, pair * PAIR * D_IN : (pair + 1) * PAIR * D_IN],
             )
 
-        for quarter in range(PAIRS):
-            quantise_weights(0, quarter, first_grouped[quarter])
+        for (n, g), tile in zip(first, first_grouped):
+            quantise_weights(n, g, tile)
         for pair in range(PAIRS):
             quantise_x(pair)
 
-        def project(n, m):
+        def project(n, pair):
             acc = psum.tile([P, BANK], F32, tag="bank", name="acc")
-            for g in range(PASSES):
-                tokens = slice((m * PASSES + g) * P, (m * PASSES + g + 1) * P)
-                nc.tensor.matmul_mx(
-                    out=acc[:],
-                    lhsT=x_codes[:, tokens].bitcast(FP8X4),
-                    lhsT_scale=x_scales[:, tokens],
-                    rhs=w_codes[:, n, g, :].bitcast(FP8X4),
-                    rhs_scale=w_scales[:, n, g, :],
-                    start=(g == 0),
-                    stop=(g == PASSES - 1),
-                )
+            for b in range(PAIR):
+                m = pair * PAIR + b
+                for g in range(PASSES):
+                    tokens = slice((m * PASSES + g) * P, (m * PASSES + g + 1) * P)
+                    nc.tensor.matmul_mx(
+                        out=acc[:, b * GROUP : (b + 1) * GROUP],
+                        lhsT=x_codes[:, tokens].bitcast(FP8X4),
+                        lhsT_scale=x_scales[:, tokens],
+                        rhs=w_codes[:, n, g, :].bitcast(FP8X4),
+                        rhs_scale=w_scales[:, n, g, :],
+                        start=(g == 0),
+                        stop=(g == PASSES - 1),
+                    )
             return acc
 
-        def sums_of_squares(acc, b, sumsq, squares, first=0):
-            for h in range(first, HEADS_PER_CHUNK):
+        def sums_of_squares(acc, i, sumsq, squares, first=0):
+            for s in range(first, SLOTS):
                 nc.scalar.activation(
-                    out=squares[:, b, h * HEAD_DIM : (h + 1) * HEAD_DIM],
-                    in_=acc[:, h * HEAD_DIM : (h + 1) * HEAD_DIM],
+                    out=squares[:, i, s * HEAD_DIM : (s + 1) * HEAD_DIM],
+                    in_=acc[:, s * HEAD_DIM : (s + 1) * HEAD_DIM],
                     func=ACT.Square,
-                    accum_out=sumsq[:, b * HEADS_PER_CHUNK + h : b * HEADS_PER_CHUNK + h + 1],
+                    accum_out=sumsq[:, i * SLOTS + s : i * SLOTS + s + 1],
                 )
 
-        def sums_of_squares_shared(acc, b, sumsq, heads):
+        def sums_of_squares_shared(acc, sumsq, count):
             squares_f32 = wide_pool.tile([P, BANK], F32, name="squares_f32")
-            width = heads * HEAD_DIM
+            width = count * HEAD_DIM
             nc.scalar.activation(out=squares_f32[:, :width], in_=acc[:, :width], func=ACT.Square)
             nc.vector.tensor_reduce(
-                out=sumsq[:, b * HEADS_PER_CHUNK : b * HEADS_PER_CHUNK + heads],
+                out=sumsq[:, :count],
                 in_=squares_f32[:, :width].rearrange("p (h d) -> p h d", d=HEAD_DIM),
                 axis=AX.X,
                 op=ALU.add,
             )
 
         def inverse_norms(sumsq):
-            inv_norm = small_pool.tile([P, PAIR * HEADS_PER_CHUNK], F32, name="inv_norm")
+            inv_norm = small_pool.tile([P, BANKS * SLOTS], F32, name="inv_norm")
             nc.scalar.activation(out=inv_norm[:], in_=sumsq[:], func=ACT.Abs_reciprocal_sqrt)
             return inv_norm
 
-        def scale(pair, b, acc, inv_norm, result):
-            nc.vector.scalar_tensor_tensor(
-                out=result[:, :, pair * PAIR + b, :],
-                in0=inv_norm[:, b * HEADS_PER_CHUNK : (b + 1) * HEADS_PER_CHUNK]
-                .unsqueeze(2)
-                .to_broadcast([P, HEADS_PER_CHUNK, HEAD_DIM]),
-                scalar=1.0 / EPS,
-                in1=acc[:].rearrange("p (h d) -> p h d", d=HEAD_DIM),
-                op0=ALU.min,
-                op1=ALU.mult,
-            )
-
-        def store(n, pair, result):
-            m1 = (pair + 1) * PAIR
-            if m1 % TOKEN_TILES_PER_STORE == 0:
-                h0 = (n % CHUNKS_PER_WEIGHT) * HEADS_PER_CHUNK
-                nc.sync.dma_start(
-                    out=out_views[n // CHUNKS_PER_WEIGHT][
-                        :, h0 : h0 + HEADS_PER_CHUNK, m1 - TOKEN_TILES_PER_STORE : m1, :
-                    ],
-                    in_=result[:, :, m1 - TOKEN_TILES_PER_STORE : m1, :],
+        def scale(i, acc, inv_norm, result):
+            for b in range(PAIR):
+                slot = i * SLOTS + b * GROUP_HEADS
+                nc.vector.scalar_tensor_tensor(
+                    out=result[:, :, i * PAIR + b, :],
+                    in0=inv_norm[:, slot : slot + GROUP_HEADS]
+                    .unsqueeze(2)
+                    .to_broadcast([P, GROUP_HEADS, HEAD_DIM]),
+                    scalar=1.0 / EPS,
+                    in1=acc[:, b * GROUP : (b + 1) * GROUP].rearrange("p (h d) -> p h d", d=HEAD_DIM),
+                    op0=ALU.min,
+                    op1=ALU.mult,
                 )
 
-        quarters = [(n, quarter) for n in range(1, CHUNKS) for quarter in range(PAIRS)]
+        def store(n, span, result):
+            h0 = (n % GROUPS_PER_WEIGHT) * GROUP_HEADS
+            nc.sync.dma_start(
+                out=out_views[n // GROUPS_PER_WEIGHT][
+                    :, h0 : h0 + GROUP_HEADS, span * SPAN : (span + 1) * SPAN, :
+                ],
+                in_=result[:],
+            )
+
+        passes = [(n, g) for n in range(GROUPS_PER_CHUNK, GROUPS) for g in range(PASSES)]
         grouped = {}
-        for i in range(VECTOR_QUARTERS, VECTOR_QUARTERS + AHEAD):
-            grouped[i] = regroup_weights_ahead(*quarters[i])
+        for i in range(VECTOR_PASSES, VECTOR_PASSES + AHEAD):
+            grouped[i] = regroup_weights_ahead(*passes[i])
 
         units = []
-        result = None
         for unit in range(UNITS + 1):
-            n, pair = divmod(unit, PAIRS)
             ready = range(unit * LEAD, (unit + 1) * LEAD) if unit < LEAD else range(unit + LEAD, unit + LEAD + 1)
-            ready = [i for i in ready if i < len(quarters)]
+            ready = [i for i in ready if i < len(passes)]
             if unit < UNITS:
-                if pair == 0:
-                    result = result_pool.tile(
-                        [P, HEADS_PER_CHUNK, TOKEN_TILES, HEAD_DIM], F32, name="result"
-                    )
-                accs = [project(n, pair * PAIR + b) for b in range(PAIR)]
-                squares = scratch_pool.tile([P, PAIR, BANK], BF16, name="squares")
-                sumsq = small_pool.tile([P, PAIR * HEADS_PER_CHUNK], F32, name="sumsq")
-                units.append((n, pair, accs, sumsq, result))
+                n, span = divmod(unit, SPANS)
+                result = result_pool.tile([P, GROUP_HEADS, SPAN, HEAD_DIM], F32, name="result")
+                accs = [project(n, span * BANKS + i) for i in range(BANKS)]
+                squares = scratch_pool.tile([P, BANKS, BANK], BF16, name="squares")
+                sumsq = small_pool.tile([P, BANKS * SLOTS], F32, name="sumsq")
+                units.append((n, span, accs, sumsq, result))
                 shared = shared_heads(unit)
                 if shared:
-                    sums_of_squares_shared(accs[0], 0, sumsq, shared)
+                    sums_of_squares_shared(accs[0], sumsq, shared)
                 sums_of_squares(accs[0], 0, sumsq, squares, shared)
             if unit > 0:
-                old_n, old_pair, old_accs, old_sumsq, old_result = units[unit - 1]
+                old_n, old_span, old_accs, old_sumsq, old_result = units[unit - 1]
                 old_inv = inverse_norms(old_sumsq)
-                scale(old_pair, 0, old_accs[0], old_inv, old_result)
+                scale(0, old_accs[0], old_inv, old_result)
             if unit < UNITS:
                 sums_of_squares(accs[1], 1, sumsq, squares)
                 for i in ready:
-                    if i < VECTOR_QUARTERS:
-                        grouped[i] = regroup_weights(*quarters[i])
+                    if i < VECTOR_PASSES:
+                        grouped[i] = regroup_weights(*passes[i])
             if unit > 0:
-                scale(old_pair, 1, old_accs[1], old_inv, old_result)
-                store(old_n, old_pair, old_result)
+                scale(1, old_accs[1], old_inv, old_result)
+                store(old_n, old_span, old_result)
             if unit < UNITS:
                 for i in ready:
-                    quantise_weights(*quarters[i], grouped[i])
-                    if VECTOR_QUARTERS <= i < len(quarters) - AHEAD:
-                        grouped[i + AHEAD] = regroup_weights_ahead(*quarters[i + AHEAD])
+                    quantise_weights(*passes[i], grouped[i])
+                    if VECTOR_PASSES <= i < len(passes) - AHEAD:
+                        grouped[i + AHEAD] = regroup_weights_ahead(*passes[i + AHEAD])

from contextlib import ExitStack

import concourse.mybir as mybir
from concourse.masks import make_identity

F32 = mybir.dt.float32
BF16 = mybir.dt.bfloat16
U32 = mybir.dt.uint32
U8 = mybir.dt.uint8
FP8X4 = mybir.dt.float8_e4m3fn_x4
ACT = mybir.ActivationFunctionType
ALU = mybir.AluOpType
AX = mybir.AxisListType

P = 128
PACK = 4
K_PASS = P * PACK

TOKENS = 1024
D_IN = 1024
FEATURES = 1024
HEAD_DIM = 64
EPS = 1e-12

PASSES = D_IN // K_PASS
TOKEN_TILES = TOKENS // P
BANK = 512
CHUNK = 512
CHUNKS_PER_WEIGHT = FEATURES // CHUNK
CHUNKS = 2 * CHUNKS_PER_WEIGHT
GROUP = 256
GROUP_HEADS = GROUP // HEAD_DIM
GROUPS_PER_WEIGHT = FEATURES // GROUP
GROUPS = 2 * GROUPS_PER_WEIGHT
GROUPS_PER_CHUNK = CHUNK // GROUP
PAIR = BANK // GROUP
PAIRS = TOKEN_TILES // PAIR
SLOTS = PAIR * GROUP_HEADS
SPAN = 4
BANKS = SPAN // PAIR
SPANS = TOKEN_TILES // SPAN
UNITS = GROUPS * SPANS
LEAD = 2
WORDS = D_IN // 2

AHEAD = 2
AHEAD_PARTS = 2
VECTOR_PASSES = 3


def shared_heads(unit):
    if unit < 3:
        return 0
    return 4 if unit < UNITS - 4 else 6


FLOPS = 2 * TOKENS * D_IN * 2 * FEATURES


def tile_attention_pa_kernel(tc, x, Wq, Wk, out_0, out_1):
    nc = tc.nc
    weights = (Wq, Wk)
    x_rows = x.flatten_outer_dims().rearrange("(p m) d -> p (m d)", m=TOKEN_TILES)
    out_views = [
        out.rearrange("b h (p m) d -> p (b h) m d", m=TOKEN_TILES) for out in (out_0, out_1)
    ]

    with ExitStack() as ctx:
        ctx.enter_context(tc.manual_schedule(engines={mybir.EngineType.DVE}))
        keep = ctx.enter_context(tc.tile_pool(name="keep", bufs=1))
        grouped_pool = ctx.enter_context(tc.tile_pool(name="grouped", bufs=4))
        ahead_pool = ctx.enter_context(tc.tile_pool(name="ahead", bufs=AHEAD))
        scratch_pool = ctx.enter_context(tc.tile_pool(name="scratch", bufs=3))
        small_pool = ctx.enter_context(tc.tile_pool(name="small", bufs=4))
        wide_pool = ctx.enter_context(tc.tile_pool(name="wide", bufs=3))
        result_pool = ctx.enter_context(tc.tile_pool(name="result", bufs=6))
        psum = ctx.enter_context(tc.psum_pool(name="psum", bufs=8))

        x_sb = keep.tile([P, TOKEN_TILES * D_IN], BF16, name="x_sb")
        w_raw = keep.tile([P, CHUNKS, PASSES, PACK, CHUNK], BF16, name="w_raw")

        def load_weights(chunk):
            w = weights[chunk // CHUNKS_PER_WEIGHT]
            c0 = (chunk % CHUNKS_PER_WEIGHT) * CHUNK
            for g in range(PASSES):
                nc.sync.dma_start(
                    out=w_raw[:, chunk, g, :, :],
                    in_=w[g * K_PASS : (g + 1) * K_PASS, c0 : c0 + CHUNK].rearrange(
                        "(p t) c -> p t c", t=PACK
                    ),
                )

        load_weights(0)
        for pair in range(PAIRS):
            cols = slice(pair * PAIR * D_IN, (pair + 1) * PAIR * D_IN)
            nc.sync.dma_start(out=x_sb[:, cols], in_=x_rows[:, cols])
        for n in range(1, CHUNKS):
            load_weights(n)

        one = keep.tile([P, 1], F32, name="one")
        nc.vector.memset(one[:], 1.0)
        warm = keep.tile([P, 1], F32, name="warm")
        nc.scalar.activation(out=warm[:], in_=one[:], func=ACT.Abs_reciprocal_sqrt)

        ident = keep.tile([P, P], F32, name="ident")
        make_identity(nc, ident[:])

        w_codes = keep.tile([P, GROUPS, PASSES, GROUP], U32, name="w_codes", align_bytes=64)
        w_scales = keep.tile([P, GROUPS, PASSES, GROUP], U8, name="w_scales", align_bytes=64)

        def weight_rows(n, g):
            c0 = (n % GROUPS_PER_CHUNK) * GROUP
            return w_raw[:, n // GROUPS_PER_CHUNK, g, :, c0 : c0 + GROUP]

        def regroup_weights_ahead(n, g):
            rows = weight_rows(n, g)
            grouped = ahead_pool.tile([P, GROUP, PACK], BF16, align_bytes=64, name="ahead")
            width = GROUP // AHEAD_PARTS
            for c in range(0, GROUP, width):
                nc.gpsimd.tensor_scalar(
                    out=grouped[:, c : c + width, :],
                    in0=rows[:, :, c : c + width].rearrange("p t c -> p c t"),
                    scalar1=1.0,
                    scalar2=0.0,
                    op0=ALU.mult,
                    op1=ALU.add,
                )
            return grouped

        def regroup_weights(n, g, on_scalar=False):
            grouped = grouped_pool.tile([P, GROUP, PACK], BF16, align_bytes=64, name="grouped")
            dst = grouped[:].rearrange("p (c i) t -> p c t i", i=4)
            rows = weight_rows(n, g).rearrange("p t (c i) -> p c t i", i=4)
            if on_scalar:
                nc.scalar.copy(out=dst, in_=rows)
            else:
                nc.vector.tensor_copy(out=dst, in_=rows)
            return grouped

        def quantise_weights(n, g, grouped):
            nc.vector.quantize_mx(
                out=w_codes[:, n, g, :].bitcast(FP8X4),
                scales=w_scales[:, n, g, :],
                in_=grouped[:].rearrange("p c t -> p (c t)"),
            )

        first = [(n, g) for g in range(PASSES) for n in range(GROUPS_PER_CHUNK)]
        first_grouped = [regroup_weights(n, g, on_scalar=((n, g) == first[-1])) for n, g in first]

        x_words = x_sb[:].bitcast(F32)
        x_grouped = keep.tile([P, TOKEN_TILES * D_IN], BF16, name="x_grouped", align_bytes=64)
        x_grouped_words = x_grouped[:].bitcast(F32)
        x_codes = keep.tile([P, TOKEN_TILES * PASSES * P], U32, name="x_codes", align_bytes=64)
        x_scales = keep.tile([P, TOKEN_TILES * PASSES * P], U8, name="x_scales", align_bytes=64)
        for pair in range(PAIRS):
            for b in range(PAIR):
                xt = psum.tile([P, BANK], F32, tag="bank", name="xt")
                m = pair * PAIR + b
                for g in range(PASSES):
                    for u in range(2):
                        nc.tensor.transpose(
                            xt[:, (2 * g + u) * P : (2 * g + u + 1) * P],
                            x_words[:, m * WORDS + 2 * P * g + u : m * WORDS + 2 * P * (g + 1) : 2],
                            ident[:],
                        )
                nc.scalar.copy(
                    out=x_grouped_words[:, m * WORDS : (m + 1) * WORDS].rearrange(
                        "p (g r u) -> p g r u", g=PASSES, u=2
                    ),
                    in_=xt[:].rearrange("p (g u r) -> p g r u", g=PASSES, u=2),
                )

        def quantise_x(pair):
            nc.vector.quantize_mx(
                out=x_codes[:, pair * PAIR * PASSES * P : (pair + 1) * PAIR * PASSES * P].bitcast(FP8X4),
                scales=x_scales[:, pair * PAIR * PASSES * P : (pair + 1) * PAIR * PASSES * P],
                in_=x_grouped[:, pair * PAIR * D_IN : (pair + 1) * PAIR * D_IN],
            )

        for (n, g), tile in zip(first, first_grouped):
            quantise_weights(n, g, tile)
        for pair in range(PAIRS):
            quantise_x(pair)

        def project(n, pair):
            acc = psum.tile([P, BANK], F32, tag="bank", name="acc")
            for b in range(PAIR):
                m = pair * PAIR + b
                for g in range(PASSES):
                    tokens = slice((m * PASSES + g) * P, (m * PASSES + g + 1) * P)
                    nc.tensor.matmul_mx(
                        out=acc[:, b * GROUP : (b + 1) * GROUP],
                        lhsT=x_codes[:, tokens].bitcast(FP8X4),
                        lhsT_scale=x_scales[:, tokens],
                        rhs=w_codes[:, n, g, :].bitcast(FP8X4),
                        rhs_scale=w_scales[:, n, g, :],
                        start=(g == 0),
                        stop=(g == PASSES - 1),
                    )
            return acc

        def sums_of_squares(acc, i, sumsq, squares, first=0):
            for s in range(first, SLOTS):
                nc.scalar.activation(
                    out=squares[:, i, s * HEAD_DIM : (s + 1) * HEAD_DIM],
                    in_=acc[:, s * HEAD_DIM : (s + 1) * HEAD_DIM],
                    func=ACT.Square,
                    accum_out=sumsq[:, i * SLOTS + s : i * SLOTS + s + 1],
                )

        def sums_of_squares_shared(acc, sumsq, count):
            squares_f32 = wide_pool.tile([P, BANK], F32, name="squares_f32")
            width = count * HEAD_DIM
            nc.scalar.activation(out=squares_f32[:, :width], in_=acc[:, :width], func=ACT.Square)
            nc.vector.tensor_reduce(
                out=sumsq[:, :count],
                in_=squares_f32[:, :width].rearrange("p (h d) -> p h d", d=HEAD_DIM),
                axis=AX.X,
                op=ALU.add,
            )

        def inverse_norms(sumsq):
            inv_norm = small_pool.tile([P, BANKS * SLOTS], F32, name="inv_norm")
            nc.scalar.activation(out=inv_norm[:], in_=sumsq[:], func=ACT.Abs_reciprocal_sqrt)
            return inv_norm

        def scale(i, acc, inv_norm, result):
            for b in range(PAIR):
                slot = i * SLOTS + b * GROUP_HEADS
                nc.vector.scalar_tensor_tensor(
                    out=result[:, :, i * PAIR + b, :],
                    in0=inv_norm[:, slot : slot + GROUP_HEADS]
                    .unsqueeze(2)
                    .to_broadcast([P, GROUP_HEADS, HEAD_DIM]),
                    scalar=1.0 / EPS,
                    in1=acc[:, b * GROUP : (b + 1) * GROUP].rearrange("p (h d) -> p h d", d=HEAD_DIM),
                    op0=ALU.min,
                    op1=ALU.mult,
                )

        def store(n, span, result):
            h0 = (n % GROUPS_PER_WEIGHT) * GROUP_HEADS
            nc.sync.dma_start(
                out=out_views[n // GROUPS_PER_WEIGHT][
                    :, h0 : h0 + GROUP_HEADS, span * SPAN : (span + 1) * SPAN, :
                ],
                in_=result[:],
            )

        passes = [(n, g) for n in range(GROUPS_PER_CHUNK, GROUPS) for g in range(PASSES)]
        grouped = {}
        for i in range(VECTOR_PASSES, VECTOR_PASSES + AHEAD):
            grouped[i] = regroup_weights_ahead(*passes[i])

        units = []
        for unit in range(UNITS + 1):
            ready = range(unit * LEAD, (unit + 1) * LEAD) if unit < LEAD else range(unit + LEAD, unit + LEAD + 1)
            ready = [i for i in ready if i < len(passes)]
            if unit < UNITS:
                n, span = divmod(unit, SPANS)
                result = result_pool.tile([P, GROUP_HEADS, SPAN, HEAD_DIM], F32, name="result")
                accs = [project(n, span * BANKS + i) for i in range(BANKS)]
                squares = scratch_pool.tile([P, BANKS, BANK], BF16, name="squares")
                sumsq = small_pool.tile([P, BANKS * SLOTS], F32, name="sumsq")
                units.append((n, span, accs, sumsq, result))
                shared = shared_heads(unit)
                if shared:
                    sums_of_squares_shared(accs[0], sumsq, shared)
                sums_of_squares(accs[0], 0, sumsq, squares, shared)
            if unit > 0:
                old_n, old_span, old_accs, old_sumsq, old_result = units[unit - 1]
                old_inv = inverse_norms(old_sumsq)
                scale(0, old_accs[0], old_inv, old_result)
            if unit < UNITS:
                sums_of_squares(accs[1], 1, sumsq, squares)
                for i in ready:
                    if i < VECTOR_PASSES:
                        grouped[i] = regroup_weights(*passes[i])
            if unit > 0:
                scale(1, old_accs[1], old_inv, old_result)
                store(old_n, old_span, old_result)
            if unit < UNITS:
                for i in ready:
                    quantise_weights(*passes[i], grouped[i])
                    if VECTOR_PASSES <= i < len(passes) - AHEAD:
                        grouped[i + AHEAD] = regroup_weights_ahead(*passes[i + AHEAD])
